import numpy as np
import ml_dtypes


def mxq(x, axis, fmt="e4m3"):
    dtype, down = {"e4m3": (ml_dtypes.float8_e4m3fn, 7), "e5m2": (ml_dtypes.float8_e5m2, 14)}[fmt]
    v = np.moveaxis(np.asarray(x, np.float32).astype(ml_dtypes.bfloat16).astype(np.float64), axis, -1)
    blocks = v.reshape(v.shape[:-1] + (-1, 32))
    amax = np.abs(blocks).max(-1, keepdims=True)
    byte = np.maximum(np.where(amax > 0, np.frexp(amax)[1] - 1 + 127, 0) - down, 1)
    scale = np.exp2(byte - 127.0)
    codes = (blocks / scale).astype(np.float32).astype(dtype).astype(np.float64)
    return np.moveaxis((codes * scale).reshape(v.shape), -1, axis)


WIDE = False


def mx_kscale(k):
    if not WIDE:
        return np.ones(k)
    levels = np.array([10, -10, 5, -5, 0])
    if k % 512:
        return np.exp2(np.random.permutation(np.resize(levels, k // 32))).repeat(32)
    a = np.empty((k // 512, 16))
    for p in range(k // 512):
        a[p, :8] = np.random.permutation(np.resize(levels, 8))
        for g in range(8):
            far = levels[np.abs(levels - a[p, g]) >= 10]
            a[p, g + 8] = far[np.random.randint(len(far))]
    return np.exp2(a.ravel()).repeat(32)


BF16 = ml_dtypes.bfloat16


def bf(x):
    return np.asarray(x, np.float32).astype(BF16)


def f64(x):
    return np.asarray(x).astype(np.float64)


B, N, DIM, H, D, M = 2, 512, 1024, 16, 64, 16
HD = H * D


def sigmoid(v):
    return 1.0 / (1.0 + np.exp(-v))


def setup_inputs():
    s = mx_kscale(DIM)
    t = mx_kscale(HD)
    return {"attn_out": bf(np.random.standard_normal((B, H, N, D)) * 0.2 * t.reshape(H, 1, D)[None]),
            "hg_lin": bf(np.random.standard_normal((B, N, H))),
            "x": bf(np.random.standard_normal((B, N, DIM)) * s),
            "Wg": bf(np.random.standard_normal((DIM, HD)) / np.sqrt(DIM) / s[:, None]),
            "bg": bf(np.random.standard_normal(HD) * 0.3),
            "bhg": bf(np.random.standard_normal(H) * 0.3),
            "Wo": bf(np.random.standard_normal((HD, DIM)) * 3.0 / np.sqrt(HD) / t[:, None])}


def reference(attn_out, hg_lin, x, Wg, bg, bhg, Wo):
    head_gate = sigmoid(f64(hg_lin) + f64(bhg))
    o = f64(attn_out) * head_gate.transpose(0, 2, 1)[..., None]
    o = o.transpose(0, 2, 1, 3).reshape(B, N, HD)
    o = o * sigmoid((mxq(f64(x), 2, "e4m3") @ mxq(f64(Wg), 0, "e4m3")) + f64(bg))
    return mxq(o, 2, "e4m3") @ mxq(f64(Wo), 0, "e4m3")

@@ -1,0 +1,279 @@
+from contextlib import ExitStack
+
+import concourse.mybir as mybir
+from concourse.masks import make_identity
+
+FLOPS = 2 * 2 * 1024 * 1024 * 1024
+
+BF16 = mybir.dt.bfloat16
+F32 = mybir.dt.float32
+U32 = mybir.dt.uint32
+U8 = mybir.dt.uint8
+FP8X4 = mybir.dt.float8_e4m3fn_x4
+ACT = mybir.ActivationFunctionType
+ALU = mybir.AluOpType
+
+P = 128
+PACK = 4
+K_PASS = P * PACK
+B = 2
+N = 512
+J = N // P
+TILES = B * J
+DIM = 1024
+H = 16
+D = 64
+HD = H * D
+HEADS_PASS = 8
+PASSES = DIM // K_PASS
+BANK = 512
+HALVES = DIM // BANK
+
+GATE_AHEAD = 4
+TRANSPOSE_AHEAD = 2
+QUANTISE_BEHIND = 1
+PROJECT_BEHIND = 2
+VECTOR_GATED_TILES = 2
+
+
+def tile_attention_pb_kernel(tc, attn_out, hg_lin, x, Wg, bg, bhg, Wo, out):
+    nc = tc.nc
+    with ExitStack() as stack:
+        keep = stack.enter_context(tc.tile_pool(name="keep", bufs=1))
+        work = stack.enter_context(tc.tile_pool(name="work", bufs=2))
+        psum = stack.enter_context(tc.psum_pool(name="psum", bufs=4))
+
+        ident_f32 = keep.tile([P, P], F32, name="ident_f32")
+        make_identity(nc, ident_f32[:])
+
+        hg_sb = keep.tile([P, B, J * H], BF16, name="hg_sb")
+        nc.sync.dma_start(out=hg_sb[:], in_=hg_lin.rearrange("b (p j) h -> p b (j h)", j=J))
+        bhg_sb = keep.tile([P, H], BF16, name="bhg_sb")
+        nc.sync.dma_start(out=bhg_sb[:], in_=bhg.partition_broadcast(P))
+        bg_sb = keep.tile([P, PASSES, PACK], BF16, name="bg_sb")
+        nc.sync.dma_start(out=bg_sb[:], in_=bg.rearrange("(g p t) -> p g t", g=PASSES, t=PACK))
+
+        x_sb = [keep.tile([P, J * DIM], BF16, name="x_sb%d" % b) for b in range(B)]
+        attn_sb = [keep.tile([P, H, J, D], BF16, name="attn_sb%d" % b) for b in range(B)]
+        wg_raw = keep.tile([P, PASSES, PACK, HD], BF16, name="wg_raw")
+        wo_raw = keep.tile([P, PASSES, PACK, DIM], BF16, name="wo_raw")
+
+        def load_x(b):
+            nc.sync.dma_start(out=x_sb[b][:], in_=x[b].rearrange("(p j) k -> p (j k)", j=J))
+
+        def load_attn(b):
+            nc.sync.dma_start(
+                out=attn_sb[b][:].rearrange("p h j d -> p h (j d)"),
+                in_=attn_out[b].rearrange("h (p j) d -> p h (j d)", j=J),
+            )
+
+        wg_view = Wg.rearrange("(g p t) c -> g p t c", g=PASSES, t=PACK)
+        wo_view = Wo.rearrange("(g p t) c -> g p t c", g=PASSES, t=PACK)
+
+        load_x(0)
+        for g in range(PASSES):
+            nc.sync.dma_start(out=wg_raw[:, g], in_=wg_view[g])
+        load_x(1)
+        load_attn(0)
+        for g in range(PASSES):
+            nc.sync.dma_start(out=wo_raw[:, g], in_=wo_view[g])
+        load_attn(1)
+
+        hg_sum = keep.tile([P, TILES, H], F32, name="hg_sum")
+        nc.vector.tensor_tensor(
+            out=hg_sum[:],
+            in0=hg_sb[:].rearrange("p b (j h) -> p (b j) h", h=H),
+            in1=bhg_sb[:].unsqueeze(1).to_broadcast([P, TILES, H]),
+            op=ALU.add,
+        )
+        head_gate = keep.tile([P, TILES, H], F32, name="head_gate")
+        nc.scalar.activation(out=head_gate[:], in_=hg_sum[:], func=ACT.Sigmoid)
+
+        bg_col = keep.tile([P, HD // P], F32, name="bg_col")
+        nc.vector.tensor_copy(out=bg_col[:], in_=bg_sb[:].rearrange("p g t -> p (g t)"))
+
+        wg_codes = keep.tile([P, PASSES, HD], U32, name="wg_codes", align_bytes=64)
+        wg_scales = keep.tile([P, PASSES, HD], U8, name="wg_scales", align_bytes=64)
+        wo_codes = keep.tile([P, PASSES, DIM], U32, name="wo_codes", align_bytes=64)
+        wo_scales = keep.tile([P, PASSES, DIM], U8, name="wo_scales", align_bytes=64)
+        x_codes = [keep.tile([P, PASSES, N], U32, name="x_codes%d" % b, align_bytes=64) for b in range(B)]
+        x_scales = [keep.tile([P, PASSES, N], U8, name="x_scales%d" % b, align_bytes=64) for b in range(B)]
+
+        def quantise_weight(raw, codes, scales, permute):
+            pieces = [(half, g) for half in range(HALVES) for g in range(PASSES)]
+            grouped = {}
+            for i in range(len(pieces) + 1):
+                if i < len(pieces):
+                    half, g = pieces[i]
+                    grouped[i] = work.tile(
+                        [P, BANK * PACK], BF16, tag="w_grp", bufs=3, align_bytes=64, name="w_grp"
+                    )
+                    block = raw[:, g, :, half * BANK : (half + 1) * BANK]
+                    if permute:
+                        nc.vector.tensor_copy(
+                            out=grouped[i][:].rearrange("p (t m j) -> p t m j", t=PACK, j=PACK),
+                            in_=block.rearrange("p j (m t) -> p t m j", t=PACK),
+                        )
+                    else:
+                        nc.vector.tensor_copy(
+                            out=grouped[i][:].rearrange("p (c i t) -> p c t i", i=4, t=PACK),
+                            in_=block.rearrange("p t (c i) -> p c t i", i=4),
+                        )
+                if i > 0:
+                    half, g = pieces[i - 1]
+                    cols = slice(half * BANK, (half + 1) * BANK)
+                    nc.vector.quantize_mx(
+                        out=codes[:, g, cols].bitcast(FP8X4), scales=scales[:, g, cols], in_=grouped[i - 1][:]
+                    )
+
+        x_grp = {}
+
+        def transpose_x(b):
+            words = x_sb[b][:].bitcast(F32)
+            for g in range(PASSES):
+                x_grp[(b, g)] = work.tile([P, N * PACK], BF16, tag="x_grp", bufs=4, align_bytes=64, name="x_grp")
+                grouped_words = x_grp[(b, g)][:].bitcast(F32)
+                for jp in range(J // 2):
+                    xt = psum.tile([P, BANK], F32, tag="tr", name="xt")
+                    for u in range(2):
+                        for jj in range(2):
+                            first = (2 * jp + jj) * (DIM // 2) + g * (K_PASS // 2)
+                            nc.tensor.transpose(
+                                xt[:, (2 * u + jj) * P : (2 * u + jj + 1) * P],
+                                words[:, first + u : first + K_PASS // 2 : 2],
+                                ident_f32[:],
+                            )
+                    nc.scalar.copy(
+                        out=grouped_words[:, jp * BANK : (jp + 1) * BANK].rearrange("q (c u) -> q c u", u=2),
+                        in_=xt[:].rearrange("q (u c) -> q c u", u=2),
+                    )
+
+        def quantise_x(b):
+            for g in range(PASSES):
+                nc.vector.quantize_mx(
+                    out=x_codes[b][:, g, :].bitcast(FP8X4), scales=x_scales[b][:, g, :], in_=x_grp[(b, g)][:]
+                )
+
+        g_sb = {}
+
+        def feature_gate(b):
+            for g2 in range(PASSES):
+                g_sb[(b, g2)] = work.tile([P, PACK, N], F32, tag="g_sb", bufs=B * PASSES, name="g_sb")
+                for t in range(PACK):
+                    m = g2 * PACK + t
+                    rows = slice(m * P, (m + 1) * P)
+                    z = psum.tile([P, N], F32, tag="mm", name="z")
+                    for g in range(PASSES):
+                        nc.tensor.matmul_mx(
+                            out=z[:],
+                            lhsT=wg_codes[:, g, rows].bitcast(FP8X4),
+                            lhsT_scale=wg_scales[:, g, rows],
+                            rhs=x_codes[b][:, g, :].bitcast(FP8X4),
+                            rhs_scale=x_scales[b][:, g, :],
+                            start=(g == 0),
+                            stop=(g == PASSES - 1),
+                        )
+                    nc.scalar.activation(
+                        out=g_sb[(b, g2)][:, t, :], in_=z[:], func=ACT.Sigmoid, bias=bg_col[:, m : m + 1]
+                    )
+
+        o_sb = {}
+
+        def gate_heads(i):
+            b, j = divmod(i, J)
+            o_sb[i] = work.tile([P, PASSES, PACK, P], F32, tag="o_sb", bufs=GATE_AHEAD + 2, name="o_sb")
+            if i < VECTOR_GATED_TILES:
+                for g2 in range(PASSES):
+                    heads = slice(g2 * HEADS_PASS, (g2 + 1) * HEADS_PASS)
+                    nc.vector.tensor_tensor(
+                        out=o_sb[i][:, g2].rearrange("p t (h m) -> p t h m", h=HEADS_PASS),
+                        in0=attn_sb[b][:, heads, j, :].rearrange("p h (m t) -> p t h m", t=PACK),
+                        in1=head_gate[:, i, heads]
+                        .unsqueeze(1)
+                        .unsqueeze(3)
+                        .to_broadcast([P, PACK, HEADS_PASS, D // PACK]),
+                        op=ALU.mult,
+                    )
+            else:
+                for h in range(H):
+                    g2, h8 = divmod(h, HEADS_PASS)
+                    nc.scalar.activation(
+                        out=o_sb[i][:, g2, :, h8 * (D // PACK) : (h8 + 1) * (D // PACK)],
+                        in_=attn_sb[b][:, h, j, :].rearrange("p (m t) -> p t m", t=PACK),
+                        func=ACT.Copy,
+                        scale=head_gate[:, i, h : h + 1],
+                    )
+
+        o_t = {}
+
+        def transpose_o(i):
+            for g2 in range(PASSES):
+                o_t[(i, g2)] = psum.tile([P, BANK], F32, tag="tr", name="o_t")
+                for t in range(PACK):
+                    nc.tensor.transpose(o_t[(i, g2)][:, t * P : (t + 1) * P], o_sb[i][:, g2, t, :], ident_f32[:])
+
+        y_grp = {}
+
+        def gate_features(i):
+            b, j = divmod(i, J)
+            y_grp[i] = work.tile([P, PASSES * P * PACK], BF16, tag="y_grp", bufs=3, align_bytes=64, name="y_grp")
+            for g2 in range(PASSES):
+                nc.vector.tensor_tensor(
+                    out=y_grp[i][:, g2 * P * PACK : (g2 + 1) * P * PACK].rearrange("p (c t) -> p c t", t=PACK),
+                    in0=o_t[(i, g2)][:].rearrange("p (t c) -> p c t", t=PACK),
+                    in1=g_sb[(b, g2)][:, :, j * P : (j + 1) * P].rearrange("p t c -> p c t"),
+                    op=ALU.mult,
+                )
+
+        y_codes = {}
+        y_scales = {}
+
+        def quantise_y(i):
+            y_codes[i] = work.tile([P, PASSES * P], U32, tag="y_codes", bufs=4, align_bytes=64, name="y_codes")
+            y_scales[i] = work.tile([P, PASSES * P], U8, tag="y_scales", bufs=4, align_bytes=64, name="y_scales")
+            nc.vector.quantize_mx(out=y_codes[i][:].bitcast(FP8X4), scales=y_scales[i][:], in_=y_grp[i][:])
+
+        def project(i):
+            b, j = divmod(i, J)
+            out_view = out[b].rearrange("(p j) c -> p j c", j=J)
+            for half in range(HALVES):
+                cols = slice(half * BANK, (half + 1) * BANK)
+                acc = psum.tile([P, BANK], F32, tag="mm", name="acc")
+                for g2 in range(PASSES):
+                    toks = slice(g2 * P, (g2 + 1) * P)
+                    nc.tensor.matmul_mx(
+                        out=acc[:],
+                        lhsT=y_codes[i][:, toks].bitcast(FP8X4),
+                        lhsT_scale=y_scales[i][:, toks],
+                        rhs=wo_codes[:, g2, cols].bitcast(FP8X4),
+                        rhs_scale=wo_scales[:, g2, cols],
+                        start=(g2 == 0),
+                        stop=(g2 == PASSES - 1),
+                    )
+                res = work.tile([P, BANK], F32, tag="res", bufs=6)
+                nc.scalar.copy(out=res[:], in_=acc[:])
+                nc.sync.dma_start(out=out_view[:, j, cols], in_=res[:])
+
+        transpose_x(0)
+        quantise_x(0)
+        quantise_weight(wg_raw, wg_codes, wg_scales, True)
+        transpose_x(1)
+        quantise_x(1)
+        feature_gate(0)
+        feature_gate(1)
+        for i in range(GATE_AHEAD):
+            gate_heads(i)
+        quantise_weight(wo_raw, wo_codes, wo_scales, False)
+        for i in range(TRANSPOSE_AHEAD):
+            transpose_o(i)
+        for i in range(TILES + PROJECT_BEHIND):
+            if i + GATE_AHEAD < TILES:
+                gate_heads(i + GATE_AHEAD)
+            if i + TRANSPOSE_AHEAD < TILES:
+                transpose_o(i + TRANSPOSE_AHEAD)
+            if i < TILES:
+                gate_features(i)
+            if 0 <= i - QUANTISE_BEHIND < TILES:
+                quantise_y(i - QUANTISE_BEHIND)
+            if i >= PROJECT_BEHIND:
+                project(i - PROJECT_BEHIND)

@@ -24,16 +24,12 @@ DIM = 1024
 H = 16
 D = 64
 HD = H * D
-HEADS_PASS = 8
+HEADS_PASS = H // 2
 PASSES = DIM // K_PASS
 BANK = 512
 HALVES = DIM // BANK
 
-GATE_AHEAD = 4
-TRANSPOSE_AHEAD = 2
-QUANTISE_BEHIND = 1
-PROJECT_BEHIND = 2
-VECTOR_GATED_TILES = 2
+VECTOR_GATED_TILES = (0, 1, 4)
 
 
 def tile_attention_pb_kernel(tc, attn_out, hg_lin, x, Wg, bg, bhg, Wo, out):
@@ -42,24 +38,38 @@ def tile_attention_pb_kernel(tc, attn_out, hg_lin, x, Wg, bg, bhg, Wo, out):
         keep = stack.enter_context(tc.tile_pool(name="keep", bufs=1))
         work = stack.enter_context(tc.tile_pool(name="work", bufs=2))
         psum = stack.enter_context(tc.psum_pool(name="psum", bufs=4))
-
-        ident_f32 = keep.tile([P, P], F32, name="ident_f32")
-        make_identity(nc, ident_f32[:])
-
-        hg_sb = keep.tile([P, B, J * H], BF16, name="hg_sb")
-        nc.sync.dma_start(out=hg_sb[:], in_=hg_lin.rearrange("b (p j) h -> p b (j h)", j=J))
-        bhg_sb = keep.tile([P, H], BF16, name="bhg_sb")
-        nc.sync.dma_start(out=bhg_sb[:], in_=bhg.partition_broadcast(P))
-        bg_sb = keep.tile([P, PASSES, PACK], BF16, name="bg_sb")
-        nc.sync.dma_start(out=bg_sb[:], in_=bg.rearrange("(g p t) -> p g t", g=PASSES, t=PACK))
+        stack.enter_context(tc.manual_schedule())
 
         x_sb = [keep.tile([P, J * DIM], BF16, name="x_sb%d" % b) for b in range(B)]
         attn_sb = [keep.tile([P, H, J, D], BF16, name="attn_sb%d" % b) for b in range(B)]
-        wg_raw = keep.tile([P, PASSES, PACK, HD], BF16, name="wg_raw")
-        wo_raw = keep.tile([P, PASSES, PACK, DIM], BF16, name="wo_raw")
+        wg_raw = {}
+        wo_raw = {}
+        for half in range(HALVES):
+            for g in range(PASSES):
+                wg_raw[(half, g)] = keep.tile([P, PACK, BANK], BF16, name="wg_raw%d%d" % (half, g))
+                wo_raw[(half, g)] = keep.tile([P, PACK, BANK], BF16, name="wo_raw%d%d" % (half, g))
+        hg_sb = keep.tile([P, B, J * H], BF16, name="hg_sb")
+        bhg_rows = keep.tile([P, H], BF16, name="bhg_rows")
+        bg_sb = keep.tile([P, PASSES * PACK], BF16, name="bg_sb")
+        ones = keep.tile([P, P], BF16, name="ones")
+        warm = keep.tile([P, 1], F32, name="warm")
 
-        def load_x(b):
-            nc.sync.dma_start(out=x_sb[b][:], in_=x[b].rearrange("(p j) k -> p (j k)", j=J))
+        nc.vector.memset(bhg_rows[:], 0.0)
+        nc.vector.memset(warm[:], 0.0)
+        nc.vector.memset(ones[:], 1.0)
+
+        wg_view = Wg.rearrange("(g p t) c -> g p t c", g=PASSES, t=PACK)
+        wo_view = Wo.rearrange("(g p t) c -> g p t c", g=PASSES, t=PACK)
+
+        def load_weight(raw, view, half, g):
+            cols = slice(half * BANK, (half + 1) * BANK)
+            nc.sync.dma_start(out=raw[(half, g)][:], in_=view[g][:, :, cols])
+
+        def load_x(b, jp):
+            nc.sync.dma_start(
+                out=x_sb[b][:, jp * 2 * DIM : (jp + 1) * 2 * DIM],
+                in_=x[b].rearrange("(p jp jj) k -> jp p (jj k)", jp=J // 2, jj=2)[jp],
+            )
 
         def load_attn(b):
             nc.sync.dma_start(
@@ -67,30 +77,43 @@ def tile_attention_pb_kernel(tc, attn_out, hg_lin, x, Wg, bg, bhg, Wo, out):
                 in_=attn_out[b].rearrange("h (p j) d -> p h (j d)", j=J),
             )
 
-        wg_view = Wg.rearrange("(g p t) c -> g p t c", g=PASSES, t=PACK)
-        wo_view = Wo.rearrange("(g p t) c -> g p t c", g=PASSES, t=PACK)
-
-        load_x(0)
-        for g in range(PASSES):
-            nc.sync.dma_start(out=wg_raw[:, g], in_=wg_view[g])
-        load_x(1)
+        load_weight(wg_raw, wg_view, 0, 0)
+        load_x(0, 0)
+        load_weight(wg_raw, wg_view, 0, 1)
+        load_x(0, 1)
+        load_x(1, 0)
+        load_x(1, 1)
+        load_weight(wg_raw, wg_view, 1, 0)
+        load_weight(wg_raw, wg_view, 1, 1)
         load_attn(0)
-        for g in range(PASSES):
-            nc.sync.dma_start(out=wo_raw[:, g], in_=wo_view[g])
+        load_weight(wo_raw, wo_view, 0, 0)
+        load_weight(wo_raw, wo_view, 0, 1)
         load_attn(1)
-
-        hg_sum = keep.tile([P, TILES, H], F32, name="hg_sum")
-        nc.vector.tensor_tensor(
-            out=hg_sum[:],
-            in0=hg_sb[:].rearrange("p b (j h) -> p (b j) h", h=H),
-            in1=bhg_sb[:].unsqueeze(1).to_broadcast([P, TILES, H]),
-            op=ALU.add,
+        load_weight(wo_raw, wo_view, 1, 0)
+        load_weight(wo_raw, wo_view, 1, 1)
+        nc.scalar.dma_start(out=hg_sb[:], in_=hg_lin.rearrange("b (p j) h -> p b (j h)", j=J))
+        nc.scalar.dma_start(out=bhg_rows[0:1, :], in_=bhg.unsqueeze(0))
+        nc.scalar.dma_start(
+            out=bg_sb[:].rearrange("p (g t) -> p g t", t=PACK), in_=bg.rearrange("(g p t) -> p g t", g=PASSES, t=PACK)
         )
-        head_gate = keep.tile([P, TILES, H], F32, name="head_gate")
-        nc.scalar.activation(out=head_gate[:], in_=hg_sum[:], func=ACT.Sigmoid)
+        nc.scalar.activation(out=warm[:], in_=warm[:], func=ACT.Sigmoid)
 
-        bg_col = keep.tile([P, HD // P], F32, name="bg_col")
-        nc.vector.tensor_copy(out=bg_col[:], in_=bg_sb[:].rearrange("p g t -> p (g t)"))
+        ident_f32 = keep.tile([P, P], F32, name="ident_f32")
+        make_identity(nc, ident_f32[:])
+
+        head_gate = keep.tile([P, TILES, H], F32, name="head_gate")
+        hg_sum = keep.tile([P, TILES, H], F32, name="hg_sum")
+
+        def compute_head_gate():
+            bhg_bc = psum.tile([P, BANK], F32, tag="mm", name="bhg_bc")
+            nc.tensor.matmul(bhg_bc[:, 0:H], lhsT=ones[:], rhs=bhg_rows[:], start=True, stop=True)
+            nc.vector.tensor_tensor(
+                out=hg_sum[:],
+                in0=hg_sb[:].rearrange("p b (j h) -> p (b j) h", h=H),
+                in1=bhg_bc[:, 0:H].unsqueeze(1).to_broadcast([P, TILES, H]),
+                op=ALU.add,
+            )
+            nc.scalar.activation(out=head_gate[:], in_=hg_sum[:], func=ACT.Sigmoid)
 
         wg_codes = keep.tile([P, PASSES, HD], U32, name="wg_codes", align_bytes=64)
         wg_scales = keep.tile([P, PASSES, HD], U8, name="wg_scales", align_bytes=64)
@@ -99,90 +122,89 @@ def tile_attention_pb_kernel(tc, attn_out, hg_lin, x, Wg, bg, bhg, Wo, out):
         x_codes = [keep.tile([P, PASSES, N], U32, name="x_codes%d" % b, align_bytes=64) for b in range(B)]
         x_scales = [keep.tile([P, PASSES, N], U8, name="x_scales%d" % b, align_bytes=64) for b in range(B)]
 
-        def quantise_weight(raw, codes, scales, permute):
-            pieces = [(half, g) for half in range(HALVES) for g in range(PASSES)]
-            grouped = {}
-            for i in range(len(pieces) + 1):
-                if i < len(pieces):
-                    half, g = pieces[i]
-                    grouped[i] = work.tile(
-                        [P, BANK * PACK], BF16, tag="w_grp", bufs=3, align_bytes=64, name="w_grp"
-                    )
-                    block = raw[:, g, :, half * BANK : (half + 1) * BANK]
-                    if permute:
-                        nc.vector.tensor_copy(
-                            out=grouped[i][:].rearrange("p (t m j) -> p t m j", t=PACK, j=PACK),
-                            in_=block.rearrange("p j (m t) -> p t m j", t=PACK),
-                        )
-                    else:
-                        nc.vector.tensor_copy(
-                            out=grouped[i][:].rearrange("p (c i t) -> p c t i", i=4, t=PACK),
-                            in_=block.rearrange("p t (c i) -> p c t i", i=4),
-                        )
-                if i > 0:
-                    half, g = pieces[i - 1]
-                    cols = slice(half * BANK, (half + 1) * BANK)
-                    nc.vector.quantize_mx(
-                        out=codes[:, g, cols].bitcast(FP8X4), scales=scales[:, g, cols], in_=grouped[i - 1][:]
-                    )
+        w_grp = {}
+
+        def group_wg(half, g):
+            w_grp[("g", half, g)] = work.tile([P, BANK * PACK], BF16, tag="w_grp", bufs=4, align_bytes=64, name="w_grp")
+            nc.vector.tensor_copy(
+                out=w_grp[("g", half, g)][:].rearrange("p (t m j) -> p t m j", t=PACK, j=PACK),
+                in_=wg_raw[(half, g)][:].rearrange("p j (m t) -> p t m j", t=PACK),
+            )
+
+        def group_wo(half, g):
+            w_grp[("o", half, g)] = work.tile([P, BANK * PACK], BF16, tag="w_grp", bufs=4, align_bytes=64, name="w_grp")
+            nc.vector.tensor_copy(
+                out=w_grp[("o", half, g)][:].rearrange("p (c i t) -> p c t i", i=4, t=PACK),
+                in_=wo_raw[(half, g)][:].rearrange("p t (c i) -> p c t i", i=4),
+            )
+
+        def quantise_wg(half, g):
+            cols = slice(half * BANK, (half + 1) * BANK)
+            nc.vector.quantize_mx(
+                out=wg_codes[:, g, cols].bitcast(FP8X4), scales=wg_scales[:, g, cols], in_=w_grp[("g", half, g)][:]
+            )
+
+        def quantise_wo(half, g):
+            cols = slice(half * BANK, (half + 1) * BANK)
+            nc.vector.quantize_mx(
+                out=wo_codes[:, g, cols].bitcast(FP8X4), scales=wo_scales[:, g, cols], in_=w_grp[("o", half, g)][:]
+            )
 
         x_grp = {}
 
-        def transpose_x(b):
+        def transpose_x(b, jp):
             words = x_sb[b][:].bitcast(F32)
             for g in range(PASSES):
-                x_grp[(b, g)] = work.tile([P, N * PACK], BF16, tag="x_grp", bufs=4, align_bytes=64, name="x_grp")
+                if jp == 0:
+                    x_grp[(b, g)] = work.tile([P, N * PACK], BF16, tag="x_grp", bufs=4, align_bytes=64, name="x_grp")
                 grouped_words = x_grp[(b, g)][:].bitcast(F32)
-                for jp in range(J // 2):
-                    xt = psum.tile([P, BANK], F32, tag="tr", name="xt")
+                xt = psum.tile([P, BANK], F32, tag="tr", name="xt")
+                for jj in range(2):
                     for u in range(2):
-                        for jj in range(2):
-                            first = (2 * jp + jj) * (DIM // 2) + g * (K_PASS // 2)
-                            nc.tensor.transpose(
-                                xt[:, (2 * u + jj) * P : (2 * u + jj + 1) * P],
-                                words[:, first + u : first + K_PASS // 2 : 2],
-                                ident_f32[:],
-                            )
-                    nc.scalar.copy(
-                        out=grouped_words[:, jp * BANK : (jp + 1) * BANK].rearrange("q (c u) -> q c u", u=2),
-                        in_=xt[:].rearrange("q (u c) -> q c u", u=2),
-                    )
-
-        def quantise_x(b):
-            for g in range(PASSES):
-                nc.vector.quantize_mx(
-                    out=x_codes[b][:, g, :].bitcast(FP8X4), scales=x_scales[b][:, g, :], in_=x_grp[(b, g)][:]
+                        first = (2 * jp + jj) * (DIM // 2) + g * (K_PASS // 2)
+                        nc.tensor.transpose(
+                            xt[:, (2 * u + jj) * P : (2 * u + jj + 1) * P],
+                            words[:, first + u : first + K_PASS // 2 : 2],
+                            ident_f32[:],
+                        )
+                nc.scalar.copy(
+                    out=grouped_words[:, jp * BANK : (jp + 1) * BANK].rearrange("q (c u) -> q c u", u=2),
+                    in_=xt[:].rearrange("q (u c) -> q c u", u=2),
                 )
+
+        def quantise_x(b, g):
+            nc.vector.quantize_mx(
+                out=x_codes[b][:, g, :].bitcast(FP8X4), scales=x_scales[b][:, g, :], in_=x_grp[(b, g)][:]
+            )
 
         g_sb = {}
 
-        def feature_gate(b):
-            for g2 in range(PASSES):
-                g_sb[(b, g2)] = work.tile([P, PACK, N], F32, tag="g_sb", bufs=B * PASSES, name="g_sb")
-                for t in range(PACK):
-                    m = g2 * PACK + t
-                    rows = slice(m * P, (m + 1) * P)
-                    z = psum.tile([P, N], F32, tag="mm", name="z")
-                    for g in range(PASSES):
-                        nc.tensor.matmul_mx(
-                            out=z[:],
-                            lhsT=wg_codes[:, g, rows].bitcast(FP8X4),
-                            lhsT_scale=wg_scales[:, g, rows],
-                            rhs=x_codes[b][:, g, :].bitcast(FP8X4),
-                            rhs_scale=x_scales[b][:, g, :],
-                            start=(g == 0),
-                            stop=(g == PASSES - 1),
-                        )
-                    nc.scalar.activation(
-                        out=g_sb[(b, g2)][:, t, :], in_=z[:], func=ACT.Sigmoid, bias=bg_col[:, m : m + 1]
+        def feature_gate(b, g2):
+            g_sb[(b, g2)] = work.tile([P, PACK, N], F32, tag="g_sb", bufs=B * PASSES, name="g_sb")
+            for t in range(PACK):
+                m = g2 * PACK + t
+                rows = slice(m * P, (m + 1) * P)
+                z = psum.tile([P, BANK], F32, tag="mm", name="z")
+                for g in range(PASSES):
+                    nc.tensor.matmul_mx(
+                        out=z[:],
+                        lhsT=wg_codes[:, g, rows].bitcast(FP8X4),
+                        lhsT_scale=wg_scales[:, g, rows],
+                        rhs=x_codes[b][:, g, :].bitcast(FP8X4),
+                        rhs_scale=x_scales[b][:, g, :],
+                        start=(g == 0),
+                        stop=(g == PASSES - 1),
                     )
+                nc.scalar.activation(
+                    out=g_sb[(b, g2)][:, t, :], in_=z[:], func=ACT.Sigmoid, bias=bg_sb[:, m : m + 1]
+                )
 
         o_sb = {}
 
         def gate_heads(i):
             b, j = divmod(i, J)
-            o_sb[i] = work.tile([P, PASSES, PACK, P], F32, tag="o_sb", bufs=GATE_AHEAD + 2, name="o_sb")
-            if i < VECTOR_GATED_TILES:
+            o_sb[i] = work.tile([P, PASSES, PACK, P], F32, tag="o_sb", bufs=TILES, name="o_sb")
+            if i in VECTOR_GATED_TILES:
                 for g2 in range(PASSES):
                     heads = slice(g2 * HEADS_PASS, (g2 + 1) * HEADS_PASS)
                     nc.vector.tensor_tensor(
@@ -233,47 +255,74 @@ def tile_attention_pb_kernel(tc, attn_out, hg_lin, x, Wg, bg, bhg, Wo, out):
             y_scales[i] = work.tile([P, PASSES * P], U8, tag="y_scales", bufs=4, align_bytes=64, name="y_scales")
             nc.vector.quantize_mx(out=y_codes[i][:].bitcast(FP8X4), scales=y_scales[i][:], in_=y_grp[i][:])
 
-        def project(i):
+        def project(i, half):
             b, j = divmod(i, J)
             out_view = out[b].rearrange("(p j) c -> p j c", j=J)
-            for half in range(HALVES):
-                cols = slice(half * BANK, (half + 1) * BANK)
-                acc = psum.tile([P, BANK], F32, tag="mm", name="acc")
-                for g2 in range(PASSES):
-                    toks = slice(g2 * P, (g2 + 1) * P)
-                    nc.tensor.matmul_mx(
-                        out=acc[:],
-                        lhsT=y_codes[i][:, toks].bitcast(FP8X4),
-                        lhsT_scale=y_scales[i][:, toks],
-                        rhs=wo_codes[:, g2, cols].bitcast(FP8X4),
-                        rhs_scale=wo_scales[:, g2, cols],
-                        start=(g2 == 0),
-                        stop=(g2 == PASSES - 1),
-                    )
-                res = work.tile([P, BANK], F32, tag="res", bufs=6)
-                nc.scalar.copy(out=res[:], in_=acc[:])
-                nc.sync.dma_start(out=out_view[:, j, cols], in_=res[:])
+            cols = slice(half * BANK, (half + 1) * BANK)
+            acc = psum.tile([P, BANK], F32, tag="mm", name="acc")
+            for g2 in range(PASSES):
+                toks = slice(g2 * P, (g2 + 1) * P)
+                nc.tensor.matmul_mx(
+                    out=acc[:],
+                    lhsT=y_codes[i][:, toks].bitcast(FP8X4),
+                    lhsT_scale=y_scales[i][:, toks],
+                    rhs=wo_codes[:, g2, cols].bitcast(FP8X4),
+                    rhs_scale=wo_scales[:, g2, cols],
+                    start=(g2 == 0),
+                    stop=(g2 == PASSES - 1),
+                )
+            res = work.tile([P, BANK], F32, tag="res", bufs=6, name="res")
+            nc.scalar.copy(out=res[:], in_=acc[:])
+            nc.sync.dma_start(out=out_view[:, j, cols], in_=res[:])
 
-        transpose_x(0)
-        quantise_x(0)
-        quantise_weight(wg_raw, wg_codes, wg_scales, True)
-        transpose_x(1)
-        quantise_x(1)
-        feature_gate(0)
-        feature_gate(1)
-        for i in range(GATE_AHEAD):
+        group_wg(0, 0)
+        transpose_x(0, 0)
+        group_wg(0, 1)
+        quantise_wg(0, 0)
+        transpose_x(0, 1)
+        quantise_wg(0, 1)
+        compute_head_gate()
+        for g in range(PASSES):
+            quantise_x(0, g)
+        transpose_x(1, 0)
+        transpose_x(1, 1)
+        group_wg(1, 0)
+        feature_gate(0, 0)
+        for g in range(PASSES):
+            quantise_x(1, g)
+        group_wg(1, 1)
+        quantise_wg(1, 0)
+        quantise_wg(1, 1)
+        feature_gate(1, 0)
+        feature_gate(0, 1)
+        gate_heads(0)
+        gate_heads(1)
+        group_wo(0, 0)
+        transpose_o(0)
+        group_wo(0, 1)
+        feature_gate(1, 1)
+        transpose_o(1)
+        quantise_wo(0, 0)
+        quantise_wo(0, 1)
+        for i in range(2, 4):
             gate_heads(i)
-        quantise_weight(wo_raw, wo_codes, wo_scales, False)
-        for i in range(TRANSPOSE_AHEAD):
-            transpose_o(i)
-        for i in range(TILES + PROJECT_BEHIND):
-            if i + GATE_AHEAD < TILES:
-                gate_heads(i + GATE_AHEAD)
-            if i + TRANSPOSE_AHEAD < TILES:
-                transpose_o(i + TRANSPOSE_AHEAD)
+
+        for i in range(TILES + 1):
+            if i + 4 < TILES:
+                gate_heads(i + 4)
             if i < TILES:
                 gate_features(i)
-            if 0 <= i - QUANTISE_BEHIND < TILES:
-                quantise_y(i - QUANTISE_BEHIND)
-            if i >= PROJECT_BEHIND:
-                project(i - PROJECT_BEHIND)
+            if i + 2 < TILES:
+                transpose_o(i + 2)
+            if i >= 1:
+                quantise_y(i - 1)
+                project(i - 1, 0)
+            if i == 1:
+                group_wo(1, 0)
+            if i == 2:
+                group_wo(1, 1)
+                quantise_wo(1, 0)
+                quantise_wo(1, 1)
+                project(0, 1)
+            if i >= 2:
+                project(i - 1, 1)

@@ -127,8 +127,8 @@ def tile_attention_pb_kernel(tc, attn_out, hg_lin, x, Wg, bg, bhg, Wo, out):
         def group_wg(half, g):
             w_grp[("g", half, g)] = work.tile([P, BANK * PACK], BF16, tag="w_grp", bufs=4, align_bytes=64, name="w_grp")
             nc.vector.tensor_copy(
-                out=w_grp[("g", half, g)][:].rearrange("p (t m j) -> p t m j", t=PACK, j=PACK),
-                in_=wg_raw[(half, g)][:].rearrange("p j (m t) -> p t m j", t=PACK),
+                out=w_grp[("g", half, g)][:].rearrange("p (t m j) -> p m j t", t=PACK, j=PACK),
+                in_=wg_raw[(half, g)][:].rearrange("p j (m t) -> p m j t", t=PACK),
             )
 
         def group_wo(half, g):
@@ -241,9 +241,9 @@ def tile_attention_pb_kernel(tc, attn_out, hg_lin, x, Wg, bg, bhg, Wo, out):
             y_grp[i] = work.tile([P, PASSES * P * PACK], BF16, tag="y_grp", bufs=3, align_bytes=64, name="y_grp")
             for g2 in range(PASSES):
                 nc.vector.tensor_tensor(
-                    out=y_grp[i][:, g2 * P * PACK : (g2 + 1) * P * PACK].rearrange("p (c t) -> p c t", t=PACK),
-                    in0=o_t[(i, g2)][:].rearrange("p (t c) -> p c t", t=PACK),
-                    in1=g_sb[(b, g2)][:, :, j * P : (j + 1) * P].rearrange("p t c -> p c t"),
+                    out=y_grp[i][:, g2 * P * PACK : (g2 + 1) * P * PACK].rearrange("p (c i t) -> p c t i", i=4, t=PACK),
+                    in0=o_t[(i, g2)][:].rearrange("p (t c i) -> p c t i", i=4, t=PACK),
+                    in1=g_sb[(b, g2)][:, :, j * P : (j + 1) * P].rearrange("p t (c i) -> p c t i", i=4),
                     op=ALU.mult,
                 )
 

@@ -29,7 +29,7 @@ PASSES = DIM // K_PASS
 BANK = 512
 HALVES = DIM // BANK
 
-VECTOR_GATED_TILES = (0, 1, 4)
+VECTOR_GATED_TILES = (0, 1)
 
 
 def tile_attention_pb_kernel(tc, attn_out, hg_lin, x, Wg, bg, bhg, Wo, out):
@@ -236,16 +236,16 @@ def tile_attention_pb_kernel(tc, attn_out, hg_lin, x, Wg, bg, bhg, Wo, out):
 
         y_grp = {}
 
-        def gate_features(i):
+        def gate_features(i, g2):
             b, j = divmod(i, J)
-            y_grp[i] = work.tile([P, PASSES * P * PACK], BF16, tag="y_grp", bufs=3, align_bytes=64, name="y_grp")
-            for g2 in range(PASSES):
-                nc.vector.tensor_tensor(
-                    out=y_grp[i][:, g2 * P * PACK : (g2 + 1) * P * PACK].rearrange("p (c i t) -> p c t i", i=4, t=PACK),
-                    in0=o_t[(i, g2)][:].rearrange("p (t c i) -> p c t i", i=4, t=PACK),
-                    in1=g_sb[(b, g2)][:, :, j * P : (j + 1) * P].rearrange("p t (c i) -> p c t i", i=4),
-                    op=ALU.mult,
-                )
+            if g2 == 0:
+                y_grp[i] = work.tile([P, PASSES * P * PACK], BF16, tag="y_grp", bufs=3, align_bytes=64, name="y_grp")
+            nc.vector.tensor_tensor(
+                out=y_grp[i][:, g2 * P * PACK : (g2 + 1) * P * PACK].rearrange("p (c i t) -> p c t i", i=4, t=PACK),
+                in0=o_t[(i, g2)][:].rearrange("p (t c i) -> p c t i", i=4, t=PACK),
+                in1=g_sb[(b, g2)][:, :, j * P : (j + 1) * P].rearrange("p t (c i) -> p c t i", i=4),
+                op=ALU.mult,
+            )
 
         y_codes = {}
         y_scales = {}
@@ -272,7 +272,10 @@ def tile_attention_pb_kernel(tc, attn_out, hg_lin, x, Wg, bg, bhg, Wo, out):
                     stop=(g2 == PASSES - 1),
                 )
             res = work.tile([P, BANK], F32, tag="res", bufs=6, name="res")
-            nc.scalar.copy(out=res[:], in_=acc[:])
+            if i == TILES - 1 and half == 1:
+                nc.vector.tensor_copy(out=res[:], in_=acc[:])
+            else:
+                nc.scalar.copy(out=res[:], in_=acc[:])
             nc.sync.dma_start(out=out_view[:, j, cols], in_=res[:])
 
         group_wg(0, 0)
@@ -307,22 +310,30 @@ def tile_attention_pb_kernel(tc, attn_out, hg_lin, x, Wg, bg, bhg, Wo, out):
         for i in range(2, 4):
             gate_heads(i)
 
+        second_half = []
         for i in range(TILES + 1):
             if i + 4 < TILES:
                 gate_heads(i + 4)
             if i < TILES:
-                gate_features(i)
+                gate_features(i, 0)
+            if i >= 1:
+                quantise_y(i - 1)
+            if i < TILES:
+                gate_features(i, 1)
             if i + 2 < TILES:
                 transpose_o(i + 2)
             if i >= 1:
-                quantise_y(i - 1)
                 project(i - 1, 0)
+                second_half.append(i - 1)
             if i == 1:
                 group_wo(1, 0)
-            if i == 2:
+            if i == 3:
                 group_wo(1, 1)
                 quantise_wo(1, 0)
                 quantise_wo(1, 1)
-                project(0, 1)
-            if i >= 2:
-                project(i - 1, 1)
+            if i >= 3:
+                for done in second_half[:2]:
+                    project(done, 1)
+                second_half = second_half[2:]
+        for done in second_half:
+            project(done, 1)

from contextlib import ExitStack

import concourse.mybir as mybir
from concourse.masks import make_identity

FLOPS = 2 * 2 * 1024 * 1024 * 1024

BF16 = mybir.dt.bfloat16
F32 = mybir.dt.float32
U32 = mybir.dt.uint32
U8 = mybir.dt.uint8
FP8X4 = mybir.dt.float8_e4m3fn_x4
ACT = mybir.ActivationFunctionType
ALU = mybir.AluOpType

P = 128
PACK = 4
K_PASS = P * PACK
B = 2
N = 512
J = N // P
TILES = B * J
DIM = 1024
H = 16
D = 64
HD = H * D
HEADS_PASS = H // 2
PASSES = DIM // K_PASS
BANK = 512
HALVES = DIM // BANK

VECTOR_GATED_TILES = (0, 1)


def tile_attention_pb_kernel(tc, attn_out, hg_lin, x, Wg, bg, bhg, Wo, out):
    nc = tc.nc
    with ExitStack() as stack:
        keep = stack.enter_context(tc.tile_pool(name="keep", bufs=1))
        work = stack.enter_context(tc.tile_pool(name="work", bufs=2))
        psum = stack.enter_context(tc.psum_pool(name="psum", bufs=4))
        stack.enter_context(tc.manual_schedule())

        x_sb = [keep.tile([P, J * DIM], BF16, name="x_sb%d" % b) for b in range(B)]
        attn_sb = [keep.tile([P, H, J, D], BF16, name="attn_sb%d" % b) for b in range(B)]
        wg_raw = {}
        wo_raw = {}
        for half in range(HALVES):
            for g in range(PASSES):
                wg_raw[(half, g)] = keep.tile([P, PACK, BANK], BF16, name="wg_raw%d%d" % (half, g))
                wo_raw[(half, g)] = keep.tile([P, PACK, BANK], BF16, name="wo_raw%d%d" % (half, g))
        hg_sb = keep.tile([P, B, J * H], BF16, name="hg_sb")
        bhg_rows = keep.tile([P, H], BF16, name="bhg_rows")
        bg_sb = keep.tile([P, PASSES * PACK], BF16, name="bg_sb")
        ones = keep.tile([P, P], BF16, name="ones")
        warm = keep.tile([P, 1], F32, name="warm")

        nc.vector.memset(bhg_rows[:], 0.0)
        nc.vector.memset(warm[:], 0.0)
        nc.vector.memset(ones[:], 1.0)

        wg_view = Wg.rearrange("(g p t) c -> g p t c", g=PASSES, t=PACK)
        wo_view = Wo.rearrange("(g p t) c -> g p t c", g=PASSES, t=PACK)

        def load_weight(raw, view, half, g):
            cols = slice(half * BANK, (half + 1) * BANK)
            nc.sync.dma_start(out=raw[(half, g)][:], in_=view[g][:, :, cols])

        def load_x(b, jp):
            nc.sync.dma_start(
                out=x_sb[b][:, jp * 2 * DIM : (jp + 1) * 2 * DIM],
                in_=x[b].rearrange("(p jp jj) k -> jp p (jj k)", jp=J // 2, jj=2)[jp],
            )

        def load_attn(b):
            nc.sync.dma_start(
                out=attn_sb[b][:].rearrange("p h j d -> p h (j d)"),
                in_=attn_out[b].rearrange("h (p j) d -> p h (j d)", j=J),
            )

        load_weight(wg_raw, wg_view, 0, 0)
        load_x(0, 0)
        load_weight(wg_raw, wg_view, 0, 1)
        load_x(0, 1)
        load_x(1, 0)
        load_x(1, 1)
        load_weight(wg_raw, wg_view, 1, 0)
        load_weight(wg_raw, wg_view, 1, 1)
        load_attn(0)
        load_weight(wo_raw, wo_view, 0, 0)
        load_weight(wo_raw, wo_view, 0, 1)
        load_attn(1)
        load_weight(wo_raw, wo_view, 1, 0)
        load_weight(wo_raw, wo_view, 1, 1)
        nc.scalar.dma_start(out=hg_sb[:], in_=hg_lin.rearrange("b (p j) h -> p b (j h)", j=J))
        nc.scalar.dma_start(out=bhg_rows[0:1, :], in_=bhg.unsqueeze(0))
        nc.scalar.dma_start(
            out=bg_sb[:].rearrange("p (g t) -> p g t", t=PACK), in_=bg.rearrange("(g p t) -> p g t", g=PASSES, t=PACK)
        )
        nc.scalar.activation(out=warm[:], in_=warm[:], func=ACT.Sigmoid)

        ident_f32 = keep.tile([P, P], F32, name="ident_f32")
        make_identity(nc, ident_f32[:])

        head_gate = keep.tile([P, TILES, H], F32, name="head_gate")
        hg_sum = keep.tile([P, TILES, H], F32, name="hg_sum")

        def compute_head_gate():
            bhg_bc = psum.tile([P, BANK], F32, tag="mm", name="bhg_bc")
            nc.tensor.matmul(bhg_bc[:, 0:H], lhsT=ones[:], rhs=bhg_rows[:], start=True, stop=True)
            nc.vector.tensor_tensor(
                out=hg_sum[:],
                in0=hg_sb[:].rearrange("p b (j h) -> p (b j) h", h=H),
                in1=bhg_bc[:, 0:H].unsqueeze(1).to_broadcast([P, TILES, H]),
                op=ALU.add,
            )
            nc.scalar.activation(out=head_gate[:], in_=hg_sum[:], func=ACT.Sigmoid)

        wg_codes = keep.tile([P, PASSES, HD], U32, name="wg_codes", align_bytes=64)
        wg_scales = keep.tile([P, PASSES, HD], U8, name="wg_scales", align_bytes=64)
        wo_codes = keep.tile([P, PASSES, DIM], U32, name="wo_codes", align_bytes=64)
        wo_scales = keep.tile([P, PASSES, DIM], U8, name="wo_scales", align_bytes=64)
        x_codes = [keep.tile([P, PASSES, N], U32, name="x_codes%d" % b, align_bytes=64) for b in range(B)]
        x_scales = [keep.tile([P, PASSES, N], U8, name="x_scales%d" % b, align_bytes=64) for b in range(B)]

        w_grp = {}

        def group_wg(half, g):
            w_grp[("g", half, g)] = work.tile([P, BANK * PACK], BF16, tag="w_grp", bufs=4, align_bytes=64, name="w_grp")
            nc.vector.tensor_copy(
                out=w_grp[("g", half, g)][:].rearrange("p (t m j) -> p m j t", t=PACK, j=PACK),
                in_=wg_raw[(half, g)][:].rearrange("p j (m t) -> p m j t", t=PACK),
            )

        def group_wo(half, g):
            w_grp[("o", half, g)] = work.tile([P, BANK * PACK], BF16, tag="w_grp", bufs=4, align_bytes=64, name="w_grp")
            nc.vector.tensor_copy(
                out=w_grp[("o", half, g)][:].rearrange("p (c i t) -> p c t i", i=4, t=PACK),
                in_=wo_raw[(half, g)][:].rearrange("p t (c i) -> p c t i", i=4),
            )

        def quantise_wg(half, g):
            cols = slice(half * BANK, (half + 1) * BANK)
            nc.vector.quantize_mx(
                out=wg_codes[:, g, cols].bitcast(FP8X4), scales=wg_scales[:, g, cols], in_=w_grp[("g", half, g)][:]
            )

        def quantise_wo(half, g):
            cols = slice(half * BANK, (half + 1) * BANK)
            nc.vector.quantize_mx(
                out=wo_codes[:, g, cols].bitcast(FP8X4), scales=wo_scales[:, g, cols], in_=w_grp[("o", half, g)][:]
            )

        x_grp = {}

        def transpose_x(b, jp):
            words = x_sb[b][:].bitcast(F32)
            for g in range(PASSES):
                if jp == 0:
                    x_grp[(b, g)] = work.tile([P, N * PACK], BF16, tag="x_grp", bufs=4, align_bytes=64, name="x_grp")
                grouped_words = x_grp[(b, g)][:].bitcast(F32)
                xt = psum.tile([P, BANK], F32, tag="tr", name="xt")
                for jj in range(2):
                    for u in range(2):
                        first = (2 * jp + jj) * (DIM // 2) + g * (K_PASS // 2)
                        nc.tensor.transpose(
                            xt[:, (2 * u + jj) * P : (2 * u + jj + 1) * P],
                            words[:, first + u : first + K_PASS // 2 : 2],
                            ident_f32[:],
                        )
                nc.scalar.copy(
                    out=grouped_words[:, jp * BANK : (jp + 1) * BANK].rearrange("q (c u) -> q c u", u=2),
                    in_=xt[:].rearrange("q (u c) -> q c u", u=2),
                )

        def quantise_x(b, g):
            nc.vector.quantize_mx(
                out=x_codes[b][:, g, :].bitcast(FP8X4), scales=x_scales[b][:, g, :], in_=x_grp[(b, g)][:]
            )

        g_sb = {}

        def feature_gate(b, g2):
            g_sb[(b, g2)] = work.tile([P, PACK, N], F32, tag="g_sb", bufs=B * PASSES, name="g_sb")
            for t in range(PACK):
                m = g2 * PACK + t
                rows = slice(m * P, (m + 1) * P)
                z = psum.tile([P, BANK], F32, tag="mm", name="z")
                for g in range(PASSES):
                    nc.tensor.matmul_mx(
                        out=z[:],
                        lhsT=wg_codes[:, g, rows].bitcast(FP8X4),
                        lhsT_scale=wg_scales[:, g, rows],
                        rhs=x_codes[b][:, g, :].bitcast(FP8X4),
                        rhs_scale=x_scales[b][:, g, :],
                        start=(g == 0),
                        stop=(g == PASSES - 1),
                    )
                nc.scalar.activation(
                    out=g_sb[(b, g2)][:, t, :], in_=z[:], func=ACT.Sigmoid, bias=bg_sb[:, m : m + 1]
                )

        o_sb = {}

        def gate_heads(i):
            b, j = divmod(i, J)
            o_sb[i] = work.tile([P, PASSES, PACK, P], F32, tag="o_sb", bufs=TILES, name="o_sb")
            if i in VECTOR_GATED_TILES:
                for g2 in range(PASSES):
                    heads = slice(g2 * HEADS_PASS, (g2 + 1) * HEADS_PASS)
                    nc.vector.tensor_tensor(
                        out=o_sb[i][:, g2].rearrange("p t (h m) -> p t h m", h=HEADS_PASS),
                        in0=attn_sb[b][:, heads, j, :].rearrange("p h (m t) -> p t h m", t=PACK),
                        in1=head_gate[:, i, heads]
                        .unsqueeze(1)
                        .unsqueeze(3)
                        .to_broadcast([P, PACK, HEADS_PASS, D // PACK]),
                        op=ALU.mult,
                    )
            else:
                for h in range(H):
                    g2, h8 = divmod(h, HEADS_PASS)
                    nc.scalar.activation(
                        out=o_sb[i][:, g2, :, h8 * (D // PACK) : (h8 + 1) * (D // PACK)],
                        in_=attn_sb[b][:, h, j, :].rearrange("p (m t) -> p t m", t=PACK),
                        func=ACT.Copy,
                        scale=head_gate[:, i, h : h + 1],
                    )

        o_t = {}

        def transpose_o(i):
            for g2 in range(PASSES):
                o_t[(i, g2)] = psum.tile([P, BANK], F32, tag="tr", name="o_t")
                for t in range(PACK):
                    nc.tensor.transpose(o_t[(i, g2)][:, t * P : (t + 1) * P], o_sb[i][:, g2, t, :], ident_f32[:])

        y_grp = {}

        def gate_features(i, g2):
            b, j = divmod(i, J)
            if g2 == 0:
                y_grp[i] = work.tile([P, PASSES * P * PACK], BF16, tag="y_grp", bufs=3, align_bytes=64, name="y_grp")
            nc.vector.tensor_tensor(
                out=y_grp[i][:, g2 * P * PACK : (g2 + 1) * P * PACK].rearrange("p (c i t) -> p c t i", i=4, t=PACK),
                in0=o_t[(i, g2)][:].rearrange("p (t c i) -> p c t i", i=4, t=PACK),
                in1=g_sb[(b, g2)][:, :, j * P : (j + 1) * P].rearrange("p t (c i) -> p c t i", i=4),
                op=ALU.mult,
            )

        y_codes = {}
        y_scales = {}

        def quantise_y(i):
            y_codes[i] = work.tile([P, PASSES * P], U32, tag="y_codes", bufs=4, align_bytes=64, name="y_codes")
            y_scales[i] = work.tile([P, PASSES * P], U8, tag="y_scales", bufs=4, align_bytes=64, name="y_scales")
            nc.vector.quantize_mx(out=y_codes[i][:].bitcast(FP8X4), scales=y_scales[i][:], in_=y_grp[i][:])

        def project(i, half):
            b, j = divmod(i, J)
            out_view = out[b].rearrange("(p j) c -> p j c", j=J)
            cols = slice(half * BANK, (half + 1) * BANK)
            acc = psum.tile([P, BANK], F32, tag="mm", name="acc")
            for g2 in range(PASSES):
                toks = slice(g2 * P, (g2 + 1) * P)
                nc.tensor.matmul_mx(
                    out=acc[:],
                    lhsT=y_codes[i][:, toks].bitcast(FP8X4),
                    lhsT_scale=y_scales[i][:, toks],
                    rhs=wo_codes[:, g2, cols].bitcast(FP8X4),
                    rhs_scale=wo_scales[:, g2, cols],
                    start=(g2 == 0),
                    stop=(g2 == PASSES - 1),
                )
            res = work.tile([P, BANK], F32, tag="res", bufs=6, name="res")
            if i == TILES - 1 and half == 1:
                nc.vector.tensor_copy(out=res[:], in_=acc[:])
            else:
                nc.scalar.copy(out=res[:], in_=acc[:])
            nc.sync.dma_start(out=out_view[:, j, cols], in_=res[:])

        group_wg(0, 0)
        transpose_x(0, 0)
        group_wg(0, 1)
        quantise_wg(0, 0)
        transpose_x(0, 1)
        quantise_wg(0, 1)
        compute_head_gate()
        for g in range(PASSES):
            quantise_x(0, g)
        transpose_x(1, 0)
        transpose_x(1, 1)
        group_wg(1, 0)
        feature_gate(0, 0)
        for g in range(PASSES):
            quantise_x(1, g)
        group_wg(1, 1)
        quantise_wg(1, 0)
        quantise_wg(1, 1)
        feature_gate(1, 0)
        feature_gate(0, 1)
        gate_heads(0)
        gate_heads(1)
        group_wo(0, 0)
        transpose_o(0)
        group_wo(0, 1)
        feature_gate(1, 1)
        transpose_o(1)
        quantise_wo(0, 0)
        quantise_wo(0, 1)
        for i in range(2, 4):
            gate_heads(i)

        second_half = []
        for i in range(TILES + 1):
            if i + 4 < TILES:
                gate_heads(i + 4)
            if i < TILES:
                gate_features(i, 0)
            if i >= 1:
                quantise_y(i - 1)
            if i < TILES:
                gate_features(i, 1)
            if i + 2 < TILES:
                transpose_o(i + 2)
            if i >= 1:
                project(i - 1, 0)
                second_half.append(i - 1)
            if i == 1:
                group_wo(1, 0)
            if i == 3:
                group_wo(1, 1)
                quantise_wo(1, 0)
                quantise_wo(1, 1)
            if i >= 3:
                for done in second_half[:2]:
                    project(done, 1)
                second_half = second_half[2:]
        for done in second_half:
            project(done, 1)
